import numpy as np
import ml_dtypes


def mxq(x, axis, fmt="e4m3"):
    dtype, down = {"e4m3": (ml_dtypes.float8_e4m3fn, 7), "e5m2": (ml_dtypes.float8_e5m2, 14)}[fmt]
    v = np.moveaxis(np.asarray(x, np.float32).astype(ml_dtypes.bfloat16).astype(np.float64), axis, -1)
    blocks = v.reshape(v.shape[:-1] + (-1, 32))
    amax = np.abs(blocks).max(-1, keepdims=True)
    byte = np.maximum(np.where(amax > 0, np.frexp(amax)[1] - 1 + 127, 0) - down, 1)
    scale = np.exp2(byte - 127.0)
    codes = (blocks / scale).astype(np.float32).astype(dtype).astype(np.float64)
    return np.moveaxis((codes * scale).reshape(v.shape), -1, axis)


WIDE = False


def mx_kscale(k):
    if not WIDE:
        return np.ones(k)
    levels = np.array([10, -10, 5, -5, 0])
    a = np.random.permutation(np.resize(levels, k // 512 * 4)).reshape(k // 512, 4)
    idx = np.arange(k)
    return np.exp2(a[idx // 512, idx % 128 // 32])


BF16 = ml_dtypes.bfloat16


def bf(x):
    return np.asarray(x, np.float32).astype(BF16)


def f64(x):
    return np.asarray(x).astype(np.float64)


E2M1 = np.array([0.0, 0.5, 1.0, 1.5, 2.0, 3.0, 4.0, 6.0, -0.0, -0.5, -1.0, -1.5, -2.0, -3.0, -4.0, -6.0])


def pack_weight(w, fmt):
    k, n = w.shape
    w = f64(bf(w)).reshape(k // 32, 32, n)
    amax = np.abs(w).max(1)
    if fmt == "e4m3":
        byte = np.frexp(amax)[1] - 1 + 127 - 7
    else:
        mant, ex = np.frexp(amax / 6.0)
        byte = np.where(mant > 0.5, ex, ex - 1) + 127
    byte = np.clip(np.where(amax > 0, byte, 1), 1, 254)
    scaled = (w * np.exp2(127.0 - byte)[:, None, :]).reshape(k, n).astype(np.float32)
    by_word = np.ascontiguousarray(scaled.reshape(k // 512, 128, 4, n).transpose(0, 1, 3, 2))
    if fmt == "e4m3":
        words = by_word.astype(ml_dtypes.float8_e4m3fn).view(np.uint8)
    else:
        c = by_word.astype(ml_dtypes.float4_e2m1fn).view(np.uint8) & 0xF
        words = c[..., 0::2] | (c[..., 1::2] << 4)
    return np.ascontiguousarray(words), np.ascontiguousarray(byte.astype(np.uint8).reshape(k // 512, 16, n))


def unpack_weight(words, scales, fmt):
    g, p, n, _ = words.shape
    if fmt == "e4m3":
        vals = np.ascontiguousarray(words).view(ml_dtypes.float8_e4m3fn).astype(np.float64)
    else:
        nib = np.empty((g, p, n, 4), np.uint8)
        nib[..., 0::2] = words & 0xF
        nib[..., 1::2] = words >> 4
        vals = E2M1[nib]
    vals = vals * np.repeat(np.exp2(scales.astype(np.float64) - 127.0), 8, axis=1)[..., None]
    return vals.transpose(0, 1, 3, 2).reshape(g * 512, n)


NB, C, O, CZ, DD, HH, WW, MG = 1, 16384, 1024, 256, 2, 2, 4, 4
STRIDES = (2, 2, 2)
FMT = "e4m3"


def setup_inputs():
    s = mx_kscale(C)
    sd, sh, sw = STRIDES
    x = bf(np.random.standard_normal((NB, C, DD, HH, WW)) * s[None, :, None, None, None])
    z = bf(np.random.standard_normal((NB, CZ, sd * DD + MG, sh * HH + MG, sw * WW + MG)))
    w_oc = np.random.standard_normal((O, C)) / np.sqrt(C) / s[None, :]
    words, scales = pack_weight(np.ascontiguousarray(w_oc.T), FMT)
    b = bf(np.random.standard_normal(O) * 0.5)
    return {"x": x, "z": z, "W_words": words, "W_scales": scales, "b": b}


def reference(x, z, W_words, W_scales, b):
    sd, sh, sw = STRIDES
    u = np.repeat(np.repeat(np.repeat(f64(x), sd, axis=2), sh, axis=3), sw, axis=4)
    n, c, d, h, w = u.shape
    y = unpack_weight(W_words, W_scales, FMT).T @ mxq(u.reshape(n, c, d * h * w), 1, "e4m3")
    y = y.reshape(n, -1, d, h, w) + f64(b)[None, :, None, None, None]
    zf = f64(z)
    off = [(zf.shape[i] - y.shape[i]) // 2 for i in range(2, 5)]
    zc = zf[:, :,
            off[0]:off[0] + y.shape[2],
            off[1]:off[1] + y.shape[3],
            off[2]:off[2] + y.shape[4]]
    return np.concatenate([y, zc], axis=1)

@@ -1,0 +1,149 @@
+from contextlib import ExitStack
+
+import concourse.mybir as mybir
+from concourse.masks import make_identity
+
+F32 = mybir.dt.float32
+BF16 = mybir.dt.bfloat16
+I32 = mybir.dt.int32
+U8 = mybir.dt.uint8
+FP8X4 = mybir.dt.float8_e4m3fn_x4
+
+P = 128
+PACK = 4
+C_IN = 16384
+GROUPS = C_IN // (P * PACK)
+C_OUT = 1024
+O_TILES = C_OUT // P
+X_POS = 16
+U_POS = 128
+C_Z = 256
+Z_PER_PART = C_Z // P
+PLANES = 4
+PLANE_GROUPS = GROUPS // PLANES
+W_LOAD_GROUPS = 2
+
+FLOPS = 2 * C_IN * C_OUT * U_POS
+
+
+def tile_upconvcropcat_k_kernel(tc, x, z, W_words, W_scales, b, out):
+    nc = tc.nc
+    out_rows = out[0].rearrange("c d y w -> c (d y w)")
+
+    with ExitStack() as ctx:
+        ctx.enter_context(tc.manual_schedule())
+        keep = ctx.enter_context(tc.tile_pool(name="keep", bufs=1))
+        psum = ctx.enter_context(tc.psum_pool(name="psum", bufs=1))
+
+        w_codes = keep.tile([P, GROUPS, C_OUT], I32, align_bytes=64)
+        w_planes = keep.tile([P, PLANE_GROUPS, C_OUT], U8, align_bytes=64)
+        x_raw = keep.tile([P, GROUPS, PACK, X_POS], BF16)
+        grouped = keep.tile([P, GROUPS, X_POS, 2, PACK], BF16, align_bytes=64)
+        q_codes = keep.tile([P, GROUPS * X_POS * 2], I32, align_bytes=64)
+        q_scales = keep.tile([P, GROUPS * X_POS * 2], U8, align_bytes=64)
+        u_codes = keep.tile([P, GROUPS, U_POS], I32, align_bytes=64)
+        u_scales = keep.tile([P, GROUPS, U_POS], U8, align_bytes=64)
+        b_rows = keep.tile([P, P], BF16)
+        ident = keep.tile([P, P], BF16)
+        bias = keep.tile([P, O_TILES], F32)
+        z_raw = keep.tile([P, Z_PER_PART, 4 * 8 * 12], BF16)
+        z_f32 = keep.tile([P, Z_PER_PART, U_POS], F32)
+        y_sb = keep.tile([P, O_TILES, U_POS], F32)
+
+        nc.vector.memset(w_planes[:].bitcast(I32), 0)
+        nc.vector.memset(q_scales[:].bitcast(I32), 0)
+        nc.vector.memset(b_rows[:], 0.0)
+
+        nc.scalar.dma_start(
+            out=x_raw[:].rearrange("p g t s -> p g (t s)"),
+            in_=x[0].rearrange("(g p t) d y w -> p g (t d y w)", p=P, t=PACK),
+        )
+        nc.scalar.dma_start(out=b_rows[0:O_TILES, :], in_=b.rearrange("(m o) -> m o", o=P))
+        nc.scalar.dma_start(
+            out=z_raw[:],
+            in_=z[0].rearrange("(p h) d y w -> p h (d y w)", h=Z_PER_PART)[:, :, 2 * 96 : 6 * 96],
+        )
+
+        scale_rows = W_scales.bitcast(I32)
+        for quadrant in range(4):
+            for r in range(4):
+                first = 32 * quadrant + r
+                nc.sync.dma_start(
+                    out=w_planes[first : first + 4 * PLANES : 4].bitcast(I32),
+                    in_=scale_rows[:, 4 * quadrant + r, :].rearrange("(j i) n -> j i n", j=PLANES),
+                )
+
+        word_rows = W_words.rearrange("g p n t -> p g (n t)").bitcast(I32)
+        for g0 in range(0, GROUPS, W_LOAD_GROUPS):
+            nc.sync.dma_start(
+                out=w_codes[:, g0 : g0 + W_LOAD_GROUPS, :],
+                in_=word_rows[:, g0 : g0 + W_LOAD_GROUPS, :],
+            )
+
+        make_identity(nc, ident[:])
+        bias_ps = psum.tile([P, P], BF16, tag="acc0")
+        nc.tensor.transpose(bias_ps[:], b_rows[:], ident[:])
+
+        for h in range(Z_PER_PART):
+            nc.scalar.copy(
+                out=z_f32[:, h, :].rearrange("p (d y w) -> p d y w", d=4, y=4),
+                in_=z_raw[:, h, :].rearrange("p (d y w) -> p d y w", d=4, y=8)[:, :, 2:6, 2:10],
+            )
+        nc.scalar.dma_start(
+            out=out_rows[C_OUT : C_OUT + C_Z, :].rearrange("(p h) s -> p h s", h=Z_PER_PART),
+            in_=z_f32[:],
+        )
+
+        nc.vector.tensor_copy(
+            out=grouped[:],
+            in_=x_raw[:].rearrange("p g t s -> p g s t").unsqueeze(3).to_broadcast([P, GROUPS, X_POS, 2, PACK]),
+        )
+        nc.vector.quantize_mx(
+            out=q_codes[:].bitcast(FP8X4),
+            scales=q_scales[:],
+            in_=grouped[:].rearrange("p g s c t -> p (g s c t)"),
+        )
+        for src, dst, width in (
+            (q_codes[:], u_codes[:].rearrange("p g s -> p (g s)"), 8),
+            (q_scales[:].bitcast(I32), u_scales[:].rearrange("p g s -> p (g s)").bitcast(I32), 2),
+        ):
+            src_view = src.rearrange("p (gd y w) -> p gd y w", y=2, w=width).unsqueeze(3)
+            dst_view = dst.rearrange("p (gd a y e w) -> p gd a y e w", a=2, y=2, e=2, w=width)
+            for a in range(2):
+                nc.vector.tensor_copy(
+                    out=dst_view[:, :, a],
+                    in_=src_view.to_broadcast([P, GROUPS * 2, 2, 2, width]),
+                )
+        nc.vector.tensor_copy(out=bias[:], in_=bias_ps[:, 0:O_TILES])
+
+        acc = [psum.tile([P, U_POS], F32, name="acc%d" % m) for m in range(O_TILES)]
+        for g in range(GROUPS):
+            plane_first = 4 * (g // PLANE_GROUPS)
+            i = g % PLANE_GROUPS
+            for m in range(O_TILES):
+                o_cols = slice(m * P, (m + 1) * P)
+                nc.tensor.matmul_mx(
+                    out=acc[m][:],
+                    lhsT=w_codes[:, g, o_cols].bitcast(FP8X4),
+                    lhsT_scale=w_planes[plane_first:P, i, o_cols],
+                    rhs=u_codes[:, g, :].bitcast(FP8X4),
+                    rhs_scale=u_scales[:, g, :],
+                    start=(g == 0),
+                    stop=(g == GROUPS - 1),
+                )
+
+        for m in range(O_TILES):
+            if m % 2 == 0:
+                nc.scalar.activation(
+                    out=y_sb[:, m, :],
+                    in_=acc[m][:],
+                    func=mybir.ActivationFunctionType.Identity,
+                    bias=bias[:, m : m + 1],
+                    scale=1.0,
+                )
+            else:
+                nc.vector.tensor_scalar_add(out=y_sb[:, m, :], in0=acc[m][:], scalar1=bias[:, m : m + 1])
+        y_rows = out_rows[0:C_OUT, :].rearrange("(m o) s -> o m s", o=P)
+        half = O_TILES // 2
+        nc.sync.dma_start(out=y_rows[:, 0:half, :], in_=y_sb[:, 0:half, :])
+        nc.sync.dma_start(out=y_rows[:, half:O_TILES, :], in_=y_sb[:, half:O_TILES, :])

@@ -64,13 +64,13 @@ def tile_upconvcropcat_k_kernel(tc, x, z, W_words, W_scales, b, out):
             in_=z[0].rearrange("(p h) d y w -> p h (d y w)", h=Z_PER_PART)[:, :, 2 * 96 : 6 * 96],
         )
 
-        scale_rows = W_scales.bitcast(I32)
-        for quadrant in range(4):
-            for r in range(4):
-                first = 32 * quadrant + r
-                nc.sync.dma_start(
-                    out=w_planes[first : first + 4 * PLANES : 4].bitcast(I32),
-                    in_=scale_rows[:, 4 * quadrant + r, :].rearrange("(j i) n -> j i n", j=PLANES),
+        make_identity(nc, ident[:])
+        scale_rows = W_scales.bitcast(F32)
+        for i in range(PLANE_GROUPS):
+            for quadrant in range(4):
+                nc.gpsimd.dma_start(
+                    out=w_planes[32 * quadrant : 32 * quadrant + 4 * PLANES, i, :].bitcast(F32),
+                    in_=scale_rows[PLANES * i : PLANES * (i + 1), 4 * quadrant : 4 * quadrant + 4, :],
                 )
 
         word_rows = W_words.rearrange("g p n t -> p g (n t)").bitcast(I32)
@@ -80,7 +80,6 @@ def tile_upconvcropcat_k_kernel(tc, x, z, W_words, W_scales, b, out):
                 in_=word_rows[:, g0 : g0 + W_LOAD_GROUPS, :],
             )
 
-        make_identity(nc, ident[:])
         bias_ps = psum.tile([P, P], BF16, tag="acc0")
         nc.tensor.transpose(bias_ps[:], b_rows[:], ident[:])
 
@@ -118,8 +117,8 @@ def tile_upconvcropcat_k_kernel(tc, x, z, W_words, W_scales, b, out):
 
         acc = [psum.tile([P, U_POS], F32, name="acc%d" % m) for m in range(O_TILES)]
         for g in range(GROUPS):
-            plane_first = 4 * (g // PLANE_GROUPS)
-            i = g % PLANE_GROUPS
+            plane_first = 4 * (g % PLANES)
+            i = g // PLANES
             for m in range(O_TILES):
                 o_cols = slice(m * P, (m + 1) * P)
                 nc.tensor.matmul_mx(

@@ -21,7 +21,7 @@ C_Z = 256
 Z_PER_PART = C_Z // P
 PLANES = 4
 PLANE_GROUPS = GROUPS // PLANES
-W_LOAD_GROUPS = 2
+W_LOADS = (2,) * 15 + (1, 1)
 
 FLOPS = 2 * C_IN * C_OUT * U_POS
 
@@ -74,11 +74,13 @@ def tile_upconvcropcat_k_kernel(tc, x, z, W_words, W_scales, b, out):
                 )
 
         word_rows = W_words.rearrange("g p n t -> p g (n t)").bitcast(I32)
-        for g0 in range(0, GROUPS, W_LOAD_GROUPS):
+        g0 = 0
+        for load_groups in W_LOADS:
             nc.sync.dma_start(
-                out=w_codes[:, g0 : g0 + W_LOAD_GROUPS, :],
-                in_=word_rows[:, g0 : g0 + W_LOAD_GROUPS, :],
+                out=w_codes[:, g0 : g0 + load_groups, :],
+                in_=word_rows[:, g0 : g0 + load_groups, :],
             )
+            g0 += load_groups
 
         bias_ps = psum.tile([P, P], BF16, tag="acc0")
         nc.tensor.transpose(bias_ps[:], b_rows[:], ident[:])
@@ -131,6 +133,7 @@ def tile_upconvcropcat_k_kernel(tc, x, z, W_words, W_scales, b, out):
                     stop=(g == GROUPS - 1),
                 )
 
+        y_rows = out_rows[0:C_OUT, :].rearrange("(m o) s -> o m s", o=P)
         for m in range(O_TILES):
             if m % 2 == 0:
                 nc.scalar.activation(
@@ -142,7 +145,4 @@ def tile_upconvcropcat_k_kernel(tc, x, z, W_words, W_scales, b, out):
                 )
             else:
                 nc.vector.tensor_scalar_add(out=y_sb[:, m, :], in0=acc[m][:], scalar1=bias[:, m : m + 1])
-        y_rows = out_rows[0:C_OUT, :].rearrange("(m o) s -> o m s", o=P)
-        half = O_TILES // 2
-        nc.sync.dma_start(out=y_rows[:, 0:half, :], in_=y_sb[:, 0:half, :])
-        nc.sync.dma_start(out=y_rows[:, half:O_TILES, :], in_=y_sb[:, half:O_TILES, :])
+                nc.sync.dma_start(out=y_rows[:, m - 1 : m + 1, :], in_=y_sb[:, m - 1 : m + 1, :])

@@ -16,12 +16,18 @@ GROUPS = C_IN // (P * PACK)
 C_OUT = 1024
 O_TILES = C_OUT // P
 X_POS = 16
+X_PAIRS = X_POS // 2
+QUADRANT = 32
+X_CHANNELS = QUADRANT * PACK
+X_WORDS = X_CHANNELS * X_PAIRS
 U_POS = 128
 C_Z = 256
 Z_PER_PART = C_Z // P
 PLANES = 4
 PLANE_GROUPS = GROUPS // PLANES
 W_LOADS = (2,) * 15 + (1, 1)
+GPSIMD_SCALES = 6
+SYNC_SCALES_AFTER = 12
 
 FLOPS = 2 * C_IN * C_OUT * U_POS
 
@@ -37,7 +43,9 @@ def tile_upconvcropcat_k_kernel(tc, x, z, W_words, W_scales, b, out):
 
         w_codes = keep.tile([P, GROUPS, C_OUT], I32, align_bytes=64)
         w_planes = keep.tile([P, PLANE_GROUPS, C_OUT], U8, align_bytes=64)
-        x_raw = keep.tile([P, GROUPS, PACK, X_POS], BF16)
+        x_rows = keep.tile([P, X_WORDS], F32, align_bytes=64)
+        x_sorted = keep.tile([P, X_WORDS], F32, align_bytes=64)
+        x_turned = keep.tile([P, X_WORDS], F32, align_bytes=64)
         grouped = keep.tile([P, GROUPS, X_POS, 2, PACK], BF16, align_bytes=64)
         q_codes = keep.tile([P, GROUPS * X_POS * 2], I32, align_bytes=64)
         q_scales = keep.tile([P, GROUPS * X_POS * 2], U8, align_bytes=64)
@@ -50,28 +58,33 @@ def tile_upconvcropcat_k_kernel(tc, x, z, W_words, W_scales, b, out):
         z_f32 = keep.tile([P, Z_PER_PART, U_POS], F32)
         y_sb = keep.tile([P, O_TILES, U_POS], F32)
 
+        nc.vector.memset(b_rows[:], 0.0)
         nc.vector.memset(w_planes[:].bitcast(I32), 0)
         nc.vector.memset(q_scales[:].bitcast(I32), 0)
-        nc.vector.memset(b_rows[:], 0.0)
 
-        nc.scalar.dma_start(
-            out=x_raw[:].rearrange("p g t s -> p g (t s)"),
-            in_=x[0].rearrange("(g p t) d y w -> p g (t d y w)", p=P, t=PACK),
-        )
-        nc.scalar.dma_start(out=b_rows[0:O_TILES, :], in_=b.rearrange("(m o) -> m o", o=P))
+        nc.sync.dma_start(out=b_rows[0:O_TILES, :], in_=b.rearrange("(m o) -> m o", o=P))
+        x_runs = x[0].rearrange("(g q c) d y w -> q g (c d y w)", q=4, c=X_CHANNELS)
+        for quadrant in range(4):
+            nc.sync.dma_start(
+                out=x_rows[QUADRANT * quadrant : QUADRANT * (quadrant + 1), :].bitcast(BF16), in_=x_runs[quadrant]
+            )
+
         nc.scalar.dma_start(
             out=z_raw[:],
             in_=z[0].rearrange("(p h) d y w -> p h (d y w)", h=Z_PER_PART)[:, :, 2 * 96 : 6 * 96],
         )
 
         make_identity(nc, ident[:])
-        scale_rows = W_scales.bitcast(F32)
-        for i in range(PLANE_GROUPS):
+
+        def load_scales(queue, dtype, i):
             for quadrant in range(4):
-                nc.gpsimd.dma_start(
-                    out=w_planes[32 * quadrant : 32 * quadrant + 4 * PLANES, i, :].bitcast(F32),
-                    in_=scale_rows[PLANES * i : PLANES * (i + 1), 4 * quadrant : 4 * quadrant + 4, :],
+                queue.dma_start(
+                    out=w_planes[QUADRANT * quadrant : QUADRANT * quadrant + 4 * PLANES, i, :].bitcast(dtype),
+                    in_=W_scales.bitcast(dtype)[PLANES * i : PLANES * (i + 1), 4 * quadrant : 4 * quadrant + 4, :],
                 )
+
+        for i in range(GPSIMD_SCALES):
+            load_scales(nc.gpsimd, F32, i)
 
         word_rows = W_words.rearrange("g p n t -> p g (n t)").bitcast(I32)
         g0 = 0
@@ -81,6 +94,9 @@ def tile_upconvcropcat_k_kernel(tc, x, z, W_words, W_scales, b, out):
                 in_=word_rows[:, g0 : g0 + load_groups, :],
             )
             g0 += load_groups
+            if g0 == SYNC_SCALES_AFTER:
+                for i in range(GPSIMD_SCALES, PLANE_GROUPS):
+                    load_scales(nc.sync, I32, i)
 
         bias_ps = psum.tile([P, P], BF16, tag="acc0")
         nc.tensor.transpose(bias_ps[:], b_rows[:], ident[:])
@@ -96,9 +112,19 @@ def tile_upconvcropcat_k_kernel(tc, x, z, W_words, W_scales, b, out):
         )
 
         nc.vector.tensor_copy(
-            out=grouped[:],
-            in_=x_raw[:].rearrange("p g t s -> p g s t").unsqueeze(3).to_broadcast([P, GROUPS, X_POS, 2, PACK]),
+            out=x_sorted[:].rearrange("p (b c) -> p b c", c=QUADRANT),
+            in_=x_rows[:].rearrange("p (c b) -> p b c", c=QUADRANT),
         )
+        nc.vector.transpose(out=x_turned[:], in_=x_sorted[:])
+        for e in range(2):
+            nc.vector.tensor_copy(
+                out=grouped[:].rearrange("p g (b e) c t -> p e b g c t", e=2)[:, e],
+                in_=x_turned[:]
+                .bitcast(BF16)
+                .rearrange("p (t b g e) -> p e b g t", t=PACK, b=X_PAIRS, e=2)[:, e]
+                .unsqueeze(3)
+                .to_broadcast([P, X_PAIRS, GROUPS, 2, PACK]),
+            )
         nc.vector.quantize_mx(
             out=q_codes[:].bitcast(FP8X4),
             scales=q_scales[:],

@@ -25,9 +25,8 @@ C_Z = 256
 Z_PER_PART = C_Z // P
 PLANES = 4
 PLANE_GROUPS = GROUPS // PLANES
-W_LOADS = (2,) * 15 + (1, 1)
-GPSIMD_SCALES = 6
-SYNC_SCALES_AFTER = 12
+W_LOADS = (4,) * 7 + (2, 1)
+LAST_LOADS = (slice(0, 6 * P), slice(6 * P, C_OUT))
 
 FLOPS = 2 * C_IN * C_OUT * U_POS
 
@@ -59,13 +58,15 @@ def tile_upconvcropcat_k_kernel(tc, x, z, W_words, W_scales, b, out):
         y_sb = keep.tile([P, O_TILES, U_POS], F32)
 
         nc.vector.memset(b_rows[:], 0.0)
-        nc.vector.memset(w_planes[:].bitcast(I32), 0)
+        for i in range(PLANE_GROUPS):
+            nc.vector.memset(w_planes[:, i, :].bitcast(I32), 0)
         nc.vector.memset(q_scales[:].bitcast(I32), 0)
 
         nc.sync.dma_start(out=b_rows[0:O_TILES, :], in_=b.rearrange("(m o) -> m o", o=P))
         x_runs = x[0].rearrange("(g q c) d y w -> q g (c d y w)", q=4, c=X_CHANNELS)
         for quadrant in range(4):
-            nc.sync.dma_start(
+            queue = nc.sync if quadrant < 2 else nc.scalar
+            queue.dma_start(
                 out=x_rows[QUADRANT * quadrant : QUADRANT * (quadrant + 1), :].bitcast(BF16), in_=x_runs[quadrant]
             )
 
@@ -75,16 +76,13 @@ def tile_upconvcropcat_k_kernel(tc, x, z, W_words, W_scales, b, out):
         )
 
         make_identity(nc, ident[:])
-
-        def load_scales(queue, dtype, i):
+        scale_rows = W_scales.bitcast(F32)
+        for i in range(PLANE_GROUPS):
             for quadrant in range(4):
-                queue.dma_start(
-                    out=w_planes[QUADRANT * quadrant : QUADRANT * quadrant + 4 * PLANES, i, :].bitcast(dtype),
-                    in_=W_scales.bitcast(dtype)[PLANES * i : PLANES * (i + 1), 4 * quadrant : 4 * quadrant + 4, :],
+                nc.gpsimd.dma_start(
+                    out=w_planes[QUADRANT * quadrant : QUADRANT * quadrant + 4 * PLANES, i, :].bitcast(F32),
+                    in_=scale_rows[PLANES * i : PLANES * (i + 1), 4 * quadrant : 4 * quadrant + 4, :],
                 )
-
-        for i in range(GPSIMD_SCALES):
-            load_scales(nc.gpsimd, F32, i)
 
         word_rows = W_words.rearrange("g p n t -> p g (n t)").bitcast(I32)
         g0 = 0
@@ -94,22 +92,11 @@ def tile_upconvcropcat_k_kernel(tc, x, z, W_words, W_scales, b, out):
                 in_=word_rows[:, g0 : g0 + load_groups, :],
             )
             g0 += load_groups
-            if g0 == SYNC_SCALES_AFTER:
-                for i in range(GPSIMD_SCALES, PLANE_GROUPS):
-                    load_scales(nc.sync, I32, i)
+        for cols in LAST_LOADS:
+            nc.sync.dma_start(out=w_codes[:, g0, cols], in_=word_rows[:, g0, cols])
 
         bias_ps = psum.tile([P, P], BF16, tag="acc0")
         nc.tensor.transpose(bias_ps[:], b_rows[:], ident[:])
-
-        for h in range(Z_PER_PART):
-            nc.scalar.copy(
-                out=z_f32[:, h, :].rearrange("p (d y w) -> p d y w", d=4, y=4),
-                in_=z_raw[:, h, :].rearrange("p (d y w) -> p d y w", d=4, y=8)[:, :, 2:6, 2:10],
-            )
-        nc.scalar.dma_start(
-            out=out_rows[C_OUT : C_OUT + C_Z, :].rearrange("(p h) s -> p h s", h=Z_PER_PART),
-            in_=z_f32[:],
-        )
 
         nc.vector.tensor_copy(
             out=x_sorted[:].rearrange("p (b c) -> p b c", c=QUADRANT),
@@ -117,7 +104,7 @@ def tile_upconvcropcat_k_kernel(tc, x, z, W_words, W_scales, b, out):
         )
         nc.vector.transpose(out=x_turned[:], in_=x_sorted[:])
         for e in range(2):
-            nc.vector.tensor_copy(
+            nc.scalar.copy(
                 out=grouped[:].rearrange("p g (b e) c t -> p e b g c t", e=2)[:, e],
                 in_=x_turned[:]
                 .bitcast(BF16)
@@ -142,6 +129,16 @@ def tile_upconvcropcat_k_kernel(tc, x, z, W_words, W_scales, b, out):
                     in_=src_view.to_broadcast([P, GROUPS * 2, 2, 2, width]),
                 )
         nc.vector.tensor_copy(out=bias[:], in_=bias_ps[:, 0:O_TILES])
+
+        for h in range(Z_PER_PART):
+            nc.scalar.copy(
+                out=z_f32[:, h, :].rearrange("p (d y w) -> p d y w", d=4, y=4),
+                in_=z_raw[:, h, :].rearrange("p (d y w) -> p d y w", d=4, y=8)[:, :, 2:6, 2:10],
+            )
+        nc.scalar.dma_start(
+            out=out_rows[C_OUT : C_OUT + C_Z, :].rearrange("(p h) s -> p h s", h=Z_PER_PART),
+            in_=z_f32[:],
+        )
 
         acc = [psum.tile([P, U_POS], F32, name="acc%d" % m) for m in range(O_TILES)]
         for g in range(GROUPS):

from contextlib import ExitStack

import concourse.mybir as mybir
from concourse.masks import make_identity

F32 = mybir.dt.float32
BF16 = mybir.dt.bfloat16
I32 = mybir.dt.int32
U8 = mybir.dt.uint8
FP8X4 = mybir.dt.float8_e4m3fn_x4

P = 128
PACK = 4
C_IN = 16384
GROUPS = C_IN // (P * PACK)
C_OUT = 1024
O_TILES = C_OUT // P
X_POS = 16
X_PAIRS = X_POS // 2
QUADRANT = 32
X_CHANNELS = QUADRANT * PACK
X_WORDS = X_CHANNELS * X_PAIRS
U_POS = 128
C_Z = 256
Z_PER_PART = C_Z // P
PLANES = 4
PLANE_GROUPS = GROUPS // PLANES
W_LOADS = (4,) * 7 + (2, 1)
LAST_LOADS = (slice(0, 6 * P), slice(6 * P, C_OUT))

FLOPS = 2 * C_IN * C_OUT * U_POS


def tile_upconvcropcat_k_kernel(tc, x, z, W_words, W_scales, b, out):
    nc = tc.nc
    out_rows = out[0].rearrange("c d y w -> c (d y w)")

    with ExitStack() as ctx:
        ctx.enter_context(tc.manual_schedule())
        keep = ctx.enter_context(tc.tile_pool(name="keep", bufs=1))
        psum = ctx.enter_context(tc.psum_pool(name="psum", bufs=1))

        w_codes = keep.tile([P, GROUPS, C_OUT], I32, align_bytes=64)
        w_planes = keep.tile([P, PLANE_GROUPS, C_OUT], U8, align_bytes=64)
        x_rows = keep.tile([P, X_WORDS], F32, align_bytes=64)
        x_sorted = keep.tile([P, X_WORDS], F32, align_bytes=64)
        x_turned = keep.tile([P, X_WORDS], F32, align_bytes=64)
        grouped = keep.tile([P, GROUPS, X_POS, 2, PACK], BF16, align_bytes=64)
        q_codes = keep.tile([P, GROUPS * X_POS * 2], I32, align_bytes=64)
        q_scales = keep.tile([P, GROUPS * X_POS * 2], U8, align_bytes=64)
        u_codes = keep.tile([P, GROUPS, U_POS], I32, align_bytes=64)
        u_scales = keep.tile([P, GROUPS, U_POS], U8, align_bytes=64)
        b_rows = keep.tile([P, P], BF16)
        ident = keep.tile([P, P], BF16)
        bias = keep.tile([P, O_TILES], F32)
        z_raw = keep.tile([P, Z_PER_PART, 4 * 8 * 12], BF16)
        z_f32 = keep.tile([P, Z_PER_PART, U_POS], F32)
        y_sb = keep.tile([P, O_TILES, U_POS], F32)

        nc.vector.memset(b_rows[:], 0.0)
        for i in range(PLANE_GROUPS):
            nc.vector.memset(w_planes[:, i, :].bitcast(I32), 0)
        nc.vector.memset(q_scales[:].bitcast(I32), 0)

        nc.sync.dma_start(out=b_rows[0:O_TILES, :], in_=b.rearrange("(m o) -> m o", o=P))
        x_runs = x[0].rearrange("(g q c) d y w -> q g (c d y w)", q=4, c=X_CHANNELS)
        for quadrant in range(4):
            queue = nc.sync if quadrant < 2 else nc.scalar
            queue.dma_start(
                out=x_rows[QUADRANT * quadrant : QUADRANT * (quadrant + 1), :].bitcast(BF16), in_=x_runs[quadrant]
            )

        nc.scalar.dma_start(
            out=z_raw[:],
            in_=z[0].rearrange("(p h) d y w -> p h (d y w)", h=Z_PER_PART)[:, :, 2 * 96 : 6 * 96],
        )

        make_identity(nc, ident[:])
        scale_rows = W_scales.bitcast(F32)
        for i in range(PLANE_GROUPS):
            for quadrant in range(4):
                nc.gpsimd.dma_start(
                    out=w_planes[QUADRANT * quadrant : QUADRANT * quadrant + 4 * PLANES, i, :].bitcast(F32),
                    in_=scale_rows[PLANES * i : PLANES * (i + 1), 4 * quadrant : 4 * quadrant + 4, :],
                )

        word_rows = W_words.rearrange("g p n t -> p g (n t)").bitcast(I32)
        g0 = 0
        for load_groups in W_LOADS:
            nc.sync.dma_start(
                out=w_codes[:, g0 : g0 + load_groups, :],
                in_=word_rows[:, g0 : g0 + load_groups, :],
            )
            g0 += load_groups
        for cols in LAST_LOADS:
            nc.sync.dma_start(out=w_codes[:, g0, cols], in_=word_rows[:, g0, cols])

        bias_ps = psum.tile([P, P], BF16, tag="acc0")
        nc.tensor.transpose(bias_ps[:], b_rows[:], ident[:])

        nc.vector.tensor_copy(
            out=x_sorted[:].rearrange("p (b c) -> p b c", c=QUADRANT),
            in_=x_rows[:].rearrange("p (c b) -> p b c", c=QUADRANT),
        )
        nc.vector.transpose(out=x_turned[:], in_=x_sorted[:])
        for e in range(2):
            nc.scalar.copy(
                out=grouped[:].rearrange("p g (b e) c t -> p e b g c t", e=2)[:, e],
                in_=x_turned[:]
                .bitcast(BF16)
                .rearrange("p (t b g e) -> p e b g t", t=PACK, b=X_PAIRS, e=2)[:, e]
                .unsqueeze(3)
                .to_broadcast([P, X_PAIRS, GROUPS, 2, PACK]),
            )
        nc.vector.quantize_mx(
            out=q_codes[:].bitcast(FP8X4),
            scales=q_scales[:],
            in_=grouped[:].rearrange("p g s c t -> p (g s c t)"),
        )
        for src, dst, width in (
            (q_codes[:], u_codes[:].rearrange("p g s -> p (g s)"), 8),
            (q_scales[:].bitcast(I32), u_scales[:].rearrange("p g s -> p (g s)").bitcast(I32), 2),
        ):
            src_view = src.rearrange("p (gd y w) -> p gd y w", y=2, w=width).unsqueeze(3)
            dst_view = dst.rearrange("p (gd a y e w) -> p gd a y e w", a=2, y=2, e=2, w=width)
            for a in range(2):
                nc.vector.tensor_copy(
                    out=dst_view[:, :, a],
                    in_=src_view.to_broadcast([P, GROUPS * 2, 2, 2, width]),
                )
        nc.vector.tensor_copy(out=bias[:], in_=bias_ps[:, 0:O_TILES])

        for h in range(Z_PER_PART):
            nc.scalar.copy(
                out=z_f32[:, h, :].rearrange("p (d y w) -> p d y w", d=4, y=4),
                in_=z_raw[:, h, :].rearrange("p (d y w) -> p d y w", d=4, y=8)[:, :, 2:6, 2:10],
            )
        nc.scalar.dma_start(
            out=out_rows[C_OUT : C_OUT + C_Z, :].rearrange("(p h) s -> p h s", h=Z_PER_PART),
            in_=z_f32[:],
        )

        acc = [psum.tile([P, U_POS], F32, name="acc%d" % m) for m in range(O_TILES)]
        for g in range(GROUPS):
            plane_first = 4 * (g % PLANES)
            i = g // PLANES
            for m in range(O_TILES):
                o_cols = slice(m * P, (m + 1) * P)
                nc.tensor.matmul_mx(
                    out=acc[m][:],
                    lhsT=w_codes[:, g, o_cols].bitcast(FP8X4),
                    lhsT_scale=w_planes[plane_first:P, i, o_cols],
                    rhs=u_codes[:, g, :].bitcast(FP8X4),
                    rhs_scale=u_scales[:, g, :],
                    start=(g == 0),
                    stop=(g == GROUPS - 1),
                )

        y_rows = out_rows[0:C_OUT, :].rearrange("(m o) s -> o m s", o=P)
        for m in range(O_TILES):
            if m % 2 == 0:
                nc.scalar.activation(
                    out=y_sb[:, m, :],
                    in_=acc[m][:],
                    func=mybir.ActivationFunctionType.Identity,
                    bias=bias[:, m : m + 1],
                    scale=1.0,
                )
            else:
                nc.vector.tensor_scalar_add(out=y_sb[:, m, :], in0=acc[m][:], scalar1=bias[:, m : m + 1])
                nc.sync.dma_start(out=y_rows[:, m - 1 : m + 1, :], in_=y_sb[:, m - 1 : m + 1, :])
